import numpy as np
import ml_dtypes


def mxq(x, axis, fmt="e4m3"):
    dtype, down = {"e4m3": (ml_dtypes.float8_e4m3fn, 7), "e5m2": (ml_dtypes.float8_e5m2, 14)}[fmt]
    v = np.moveaxis(np.asarray(x, np.float32).astype(ml_dtypes.bfloat16).astype(np.float64), axis, -1)
    blocks = v.reshape(v.shape[:-1] + (-1, 32))
    amax = np.abs(blocks).max(-1, keepdims=True)
    byte = np.maximum(np.where(amax > 0, np.frexp(amax)[1] - 1 + 127, 0) - down, 1)
    scale = np.exp2(byte - 127.0)
    codes = (blocks / scale).astype(np.float32).astype(dtype).astype(np.float64)
    return np.moveaxis((codes * scale).reshape(v.shape), -1, axis)


WIDE = False


def mx_kscale(k):
    if not WIDE:
        return np.ones(k)
    levels = np.array([10, -10, 5, -5, 0])
    a = np.random.permutation(np.resize(levels, k // 512 * 4)).reshape(k // 512, 4)
    idx = np.arange(k)
    return np.exp2(a[idx // 512, idx % 128 // 32])


BF16 = ml_dtypes.bfloat16


def bf(x):
    return np.asarray(x, np.float32).astype(BF16)


def f64(x):
    return np.asarray(x).astype(np.float64)


H, L, B, S = 1024, 2, 128, 32


def sigmoid(v):
    return 1.0 / (1.0 + np.exp(-v))


def setup_inputs():
    r = np.random.standard_normal
    s, t, u = mx_kscale(H), mx_kscale(H), mx_kscale(H)
    st = np.concatenate([s, t])
    return {
        "x": bf(r((B, H)) * s),
        "enc_seq": bf(r((S, B, H)) * t),
        "attn_W": bf(r((H, H)) / np.sqrt(H) / s[None, :] / t[:, None]),
        "attn_b": bf(r(H) * 0.5 / t),
        "h_prev": bf(r((B, H)) * u),
        "c_prev": bf(r((B, H))),
        "W_ih0": bf(r((4 * H, H + H)) * 0.6 / np.sqrt(H) / st[None, :]),
        "W_hh0": bf(r((4 * H, H)) * 0.6 / np.sqrt(H) / u[None, :]),
        "b_ih0": bf(r(4 * H) * 0.3),
        "b_hh0": bf(r(4 * H) * 0.3),
    }


def reference(x, enc_seq, attn_W, attn_b, h_prev, c_prev, W_ih0, W_hh0, b_ih0, b_hh0):
    enc = f64(enc_seq)
    xq = mxq(f64(x), 1, "e4m3")
    attn_lin = (xq @ mxq(f64(attn_W).T, 0, "e4m3")) + f64(attn_b)
    scores = attn_lin[None, :, :] * enc
    e = np.exp(scores - scores.max(0, keepdims=True))
    w = e / e.sum(0, keepdims=True)
    attention = (enc * w).sum(0)
    aq = mxq(attention, 1, "e4m3")
    w_x = mxq(f64(W_ih0)[:, :H].T, 0, "e4m3")
    w_a = mxq(f64(W_ih0)[:, H:].T, 0, "e4m3")
    hq = mxq(f64(h_prev), 1, "e4m3")
    gates = (xq @ w_x) + (aq @ w_a) + f64(b_ih0) + (hq @ mxq(f64(W_hh0).T, 0, "e4m3")) + f64(b_hh0)
    i, f, g, o = np.split(gates, 4, axis=-1)
    c_new = sigmoid(f) * f64(c_prev) + sigmoid(i) * np.tanh(g)
    h_new = sigmoid(o) * np.tanh(c_new)
    return h_new, c_new

@@ -1,0 +1,286 @@
+from contextlib import ExitStack
+
+import concourse.mybir as mybir
+from concourse.masks import make_identity
+
+F32 = mybir.dt.float32
+BF16 = mybir.dt.bfloat16
+I32 = mybir.dt.int32
+U32 = mybir.dt.uint32
+U8 = mybir.dt.uint8
+FP8X4 = mybir.dt.float8_e4m3fn_x4
+ALU = mybir.AluOpType
+ACT = mybir.ActivationFunctionType
+
+P = 128
+H = 1024
+S = 32
+K_PASS = 512
+PASS_WORDS = K_PASS // 2
+H_PASSES = H // K_PASS
+N_BLOCK = 512
+ROW_TILES = N_BLOCK // P
+GATE_BLOCKS = 4 * H // N_BLOCK
+GROUP = 256
+GROUPS = H // GROUP
+
+FLOPS = 2 * P * (H * H + 4 * H * 3 * H)
+
+
+def quantise_weight_pass(nc, psum, stage, ident, words, codes, plane):
+    grouped = stage.tile([P, 4 * N_BLOCK], BF16, tag="grouped", bufs=3, align_bytes=64)
+    grouped_words = grouped[:].bitcast(F32).rearrange("p (r u) -> p r u", u=2)
+    for pair in range(ROW_TILES // 2):
+        bank = psum.tile([P, 2, 2 * P], F32, tag="wt", bufs=4)
+        for i in range(2):
+            for u in range(2):
+                nc.tensor.transpose(
+                    bank[:, u, i * P : (i + 1) * P],
+                    words[:, 2 * pair + i, u * P : (u + 1) * P],
+                    ident[:],
+                )
+        nc.scalar.copy(
+            out=grouped_words[:, pair * 2 * P : (pair + 1) * 2 * P, :],
+            in_=bank[:].rearrange("p u r -> p r u"),
+        )
+    nc.vector.quantize_mx(out=codes.bitcast(FP8X4), scales=plane, in_=grouped[:])
+
+
+def quantise_activations(nc, psum, stage, ident, rows, codes, planes):
+    words = rows[:].bitcast(F32)
+    bank = psum.tile([P, 2 * H_PASSES, P], F32, tag="wt", bufs=4)
+    for q in range(2 * H_PASSES):
+        nc.tensor.transpose(bank[:, q, :], words[:, q * P : (q + 1) * P], ident[:])
+    grouped = stage.tile([P, 4 * H_PASSES * P], BF16, tag="act_grouped", bufs=2, align_bytes=64)
+    nc.scalar.copy(
+        out=grouped[:].bitcast(F32).rearrange("p (g b u) -> p g b u", g=H_PASSES, u=2),
+        in_=bank[:].rearrange("p (g u) b -> p g b u", u=2),
+    )
+    nc.vector.quantize_mx(
+        out=codes[:].rearrange("p g b -> p (g b)").bitcast(FP8X4),
+        scales=planes[:].rearrange("p g b -> p (g b)"),
+        in_=grouped[:],
+    )
+
+
+def tile_decoderlstm_pa_kernel(
+    tc, x, enc_seq, attn_W, attn_b, h_prev, c_prev, W_ih0, W_hh0, b_ih0, b_hh0, out_0, out_1
+):
+    nc = tc.nc
+    with ExitStack() as stack:
+        const = stack.enter_context(tc.tile_pool(name="const", bufs=1))
+        keep = stack.enter_context(tc.tile_pool(name="keep", bufs=1))
+        stage = stack.enter_context(tc.tile_pool(name="stage", bufs=2))
+        work = stack.enter_context(tc.tile_pool(name="work", bufs=2))
+        psum = stack.enter_context(tc.psum_pool(name="psum", bufs=2))
+
+        ident = const.tile([P, P], F32)
+        make_identity(nc, ident[:])
+        ones = const.tile([P, P], BF16)
+        nc.vector.memset(ones[:], 1.0)
+
+        x_sb = keep.tile([P, H], BF16)
+        nc.sync.dma_start(out=x_sb[:], in_=x)
+        bias_rows = work.tile([P, 5 * H], BF16, tag="T")
+        nc.vector.memset(bias_rows[:].bitcast(I32), 0)
+        nc.sync.dma_start(out=bias_rows[0:1, 4 * H : 5 * H], in_=attn_b.rearrange("(o n) -> o n", o=1))
+        attn_w = stage.tile([P, 2 * ROW_TILES, H], BF16, tag="wih")
+        attn_w_rows = attn_W.rearrange("(t p) k -> p t k", p=P)
+        for nb in range(H // N_BLOCK):
+            tiles = slice(nb * ROW_TILES, (nb + 1) * ROW_TILES)
+            nc.sync.dma_start(out=attn_w[:, tiles, :], in_=attn_w_rows[:, tiles, :])
+        nc.sync.dma_start(out=bias_rows[0:1, 0 : 4 * H], in_=b_ih0.rearrange("(o n) -> o n", o=1))
+        nc.sync.dma_start(out=bias_rows[1:2, 0 : 4 * H], in_=b_hh0.rearrange("(o n) -> o n", o=1))
+        h_sb = keep.tile([P, H], BF16)
+        nc.sync.dma_start(out=h_sb[:], in_=h_prev)
+        c_sb = keep.tile([P, H], BF16)
+        nc.sync.dma_start(out=c_sb[:], in_=c_prev)
+
+        attn_lin = keep.tile([P, H], F32)
+        gates_xh = keep.tile([P, 4 * H], F32)
+        for nb in range(H // N_BLOCK):
+            cols = slice(nb * N_BLOCK, (nb + 1) * N_BLOCK)
+            spread = psum.tile([P, N_BLOCK], F32, tag="acc")
+            nc.tensor.matmul(
+                out=spread[:],
+                lhsT=ones[:],
+                rhs=bias_rows[:, 4 * H + nb * N_BLOCK : 4 * H + (nb + 1) * N_BLOCK],
+                start=True,
+                stop=True,
+            )
+            nc.scalar.copy(out=attn_lin[:, cols], in_=spread[:])
+        for nb in range(GATE_BLOCKS):
+            cols = slice(nb * N_BLOCK, (nb + 1) * N_BLOCK)
+            spread = psum.tile([P, N_BLOCK], F32, tag="acc")
+            nc.tensor.matmul(out=spread[:], lhsT=ones[:], rhs=bias_rows[:, cols], start=True, stop=True)
+            nc.scalar.copy(out=gates_xh[:, cols], in_=spread[:])
+
+        x_codes = keep.tile([P, H_PASSES, P], U32, align_bytes=64)
+        x_planes = keep.tile([P, H_PASSES, P], U8, align_bytes=64)
+        quantise_activations(nc, psum, stage, ident, x_sb, x_codes, x_planes)
+        h_codes = keep.tile([P, H_PASSES, P], U32, align_bytes=64)
+        h_planes = keep.tile([P, H_PASSES, P], U8, align_bytes=64)
+        quantise_activations(nc, psum, stage, ident, h_sb, h_codes, h_planes)
+
+        attn_w_words = attn_w[:].bitcast(F32)
+        for nb in range(H // N_BLOCK):
+            cols = slice(nb * N_BLOCK, (nb + 1) * N_BLOCK)
+            acc = psum.tile([P, N_BLOCK], F32, tag="acc")
+            for g in range(H_PASSES):
+                w_codes = stage.tile([P, N_BLOCK], U32, tag="w_codes", bufs=4, align_bytes=64)
+                w_plane = stage.tile([P, N_BLOCK], U8, tag="w_plane", bufs=4, align_bytes=64)
+                quantise_weight_pass(
+                    nc, psum, stage, ident,
+                    attn_w_words[:, nb * ROW_TILES : (nb + 1) * ROW_TILES, g * PASS_WORDS : (g + 1) * PASS_WORDS],
+                    w_codes[:], w_plane[:],
+                )
+                nc.tensor.matmul_mx(
+                    out=acc[:],
+                    lhsT=x_codes[:, g, :].bitcast(FP8X4),
+                    lhsT_scale=x_planes[:, g, :],
+                    rhs=w_codes[:].bitcast(FP8X4),
+                    rhs_scale=w_plane[:],
+                    start=(g == 0),
+                    stop=(g == H_PASSES - 1),
+                )
+            nc.vector.tensor_tensor(out=attn_lin[:, cols], in0=acc[:], in1=attn_lin[:, cols], op=ALU.add)
+
+        wa_codes = keep.tile([P, GATE_BLOCKS, H_PASSES, N_BLOCK], U32, align_bytes=64)
+        wa_planes = keep.tile([P, GATE_BLOCKS, H_PASSES, N_BLOCK], U8, align_bytes=64)
+        att_codes = keep.tile([P, H_PASSES, P], U32, align_bytes=64)
+        att_planes = keep.tile([P, H_PASSES, P], U8, align_bytes=64)
+
+        def gate_block(nb):
+            rows = slice(nb * N_BLOCK, (nb + 1) * N_BLOCK)
+            w_ih = stage.tile([P, ROW_TILES, 2 * H], BF16, tag="wih")
+            nc.sync.dma_start(out=w_ih[:], in_=W_ih0[rows, :].rearrange("(t p) k -> p t k", p=P))
+            w_hh = stage.tile([P, ROW_TILES, H], BF16, tag="whh")
+            nc.sync.dma_start(out=w_hh[:], in_=W_hh0[rows, :].rearrange("(t p) k -> p t k", p=P))
+            w_ih_words = w_ih[:].bitcast(F32)
+            w_hh_words = w_hh[:].bitcast(F32)
+            acc = psum.tile([P, N_BLOCK], F32, tag="acc")
+            sources = ((w_ih_words, x_codes, x_planes), (w_hh_words, h_codes, h_planes))
+            for i, (w_words, act_codes, act_planes) in enumerate(sources):
+                for g in range(H_PASSES):
+                    w_codes = stage.tile([P, N_BLOCK], U32, tag="w_codes", bufs=4, align_bytes=64)
+                    w_plane = stage.tile([P, N_BLOCK], U8, tag="w_plane", bufs=4, align_bytes=64)
+                    quantise_weight_pass(
+                        nc, psum, stage, ident,
+                        w_words[:, :, g * PASS_WORDS : (g + 1) * PASS_WORDS],
+                        w_codes[:], w_plane[:],
+                    )
+                    nc.tensor.matmul_mx(
+                        out=acc[:],
+                        lhsT=act_codes[:, g, :].bitcast(FP8X4),
+                        lhsT_scale=act_planes[:, g, :],
+                        rhs=w_codes[:].bitcast(FP8X4),
+                        rhs_scale=w_plane[:],
+                        start=(i == 0 and g == 0),
+                        stop=(i == 1 and g == H_PASSES - 1),
+                    )
+            nc.vector.tensor_tensor(out=gates_xh[:, rows], in0=acc[:], in1=gates_xh[:, rows], op=ALU.add)
+            for g in range(H_PASSES):
+                quantise_weight_pass(
+                    nc, psum, stage, ident,
+                    w_ih_words[:, :, (H_PASSES + g) * PASS_WORDS : (H_PASSES + g + 1) * PASS_WORDS],
+                    wa_codes[:, nb, g, :], wa_planes[:, nb, g, :],
+                )
+
+        for group in range(GROUPS):
+            feats = slice(group * GROUP, (group + 1) * GROUP)
+            enc = work.tile([P, S, GROUP], BF16, tag="enc")
+            nc.sync.dma_start(out=enc[:], in_=enc_seq[:, :, feats].rearrange("s b j -> b s j"))
+
+            top = work.tile([P, S // 4, GROUP], BF16, tag="top", bufs=1)
+            low = work.tile([P, S // 4, GROUP], BF16, tag="low", bufs=1)
+            quarter = S // 4
+            nc.vector.tensor_tensor(out=top[:], in0=enc[:, 0:quarter, :], in1=enc[:, quarter : 2 * quarter, :], op=ALU.max)
+            nc.vector.tensor_tensor(out=low[:], in0=enc[:, 0:quarter, :], in1=enc[:, quarter : 2 * quarter, :], op=ALU.min)
+            for i in range(2, 4):
+                nc.vector.tensor_tensor(out=top[:], in0=top[:], in1=enc[:, i * quarter : (i + 1) * quarter, :], op=ALU.max)
+                nc.vector.tensor_tensor(out=low[:], in0=low[:], in1=enc[:, i * quarter : (i + 1) * quarter, :], op=ALU.min)
+            half = quarter // 2
+            while half >= 1:
+                nc.vector.tensor_tensor(out=top[:, 0:half, :], in0=top[:, 0:half, :], in1=top[:, half : 2 * half, :], op=ALU.max)
+                nc.vector.tensor_tensor(out=low[:, 0:half, :], in0=low[:, 0:half, :], in1=low[:, half : 2 * half, :], op=ALU.min)
+                half //= 2
+            at_top = work.tile([P, GROUP], F32, tag="at_top")
+            at_low = work.tile([P, GROUP], F32, tag="at_low")
+            peak = work.tile([P, GROUP], F32, tag="peak")
+            nc.vector.tensor_tensor(out=at_top[:], in0=attn_lin[:, feats], in1=top[:, 0, :], op=ALU.mult)
+            nc.vector.tensor_tensor(out=at_low[:], in0=attn_lin[:, feats], in1=low[:, 0, :], op=ALU.mult)
+            nc.vector.tensor_tensor(out=peak[:], in0=at_top[:], in1=at_low[:], op=ALU.max)
+
+            g, u = divmod(group, 2)
+            if u == 0:
+                att_t = work.tile([P, 4, P], F32, tag="att_t")
+            for e in range(2):
+                enc_c = enc[:].rearrange("b s (p e) -> b s e p", e=2)[:, :, e, :]
+                lin_c = attn_lin[:, feats].rearrange("b (p e) -> b e p", e=2)[:, e, :]
+                peak_c = peak[:].rearrange("b (p e) -> b e p", e=2)[:, e, :]
+                terms = work.tile([P, S, P], F32, tag="T")
+                nc.vector.tensor_tensor(
+                    out=terms[:], in0=enc_c, in1=lin_c.unsqueeze(1).to_broadcast([P, S, P]), op=ALU.mult
+                )
+                nc.vector.tensor_tensor(
+                    out=terms[:], in0=terms[:], in1=peak_c.unsqueeze(1).to_broadcast([P, S, P]), op=ALU.subtract
+                )
+                nc.scalar.activation(out=terms[:], in_=terms[:], func=ACT.Exp)
+                sums = psum.tile([P, 2, P], F32, tag="sums")
+                for s in range(S):
+                    nc.tensor.matmul(
+                        out=sums[:, 0, :], lhsT=terms[:, s, :], rhs=ident[:], is_transpose=True,
+                        start=(s == 0), stop=(s == S - 1),
+                    )
+                nc.vector.tensor_tensor(out=terms[:], in0=terms[:], in1=enc_c, op=ALU.mult)
+                for s in range(S):
+                    nc.tensor.matmul(
+                        out=sums[:, 1, :], lhsT=terms[:, s, :], rhs=ident[:], is_transpose=True,
+                        start=(s == 0), stop=(s == S - 1),
+                    )
+                inverse = work.tile([P, P], F32, tag="inverse")
+                nc.vector.reciprocal(out=inverse[:], in_=sums[:, 0, :])
+                nc.vector.tensor_tensor(out=att_t[:, 2 * u + e, :], in0=sums[:, 1, :], in1=inverse[:], op=ALU.mult)
+
+                gate_block(2 * group + e)
+
+            if u == 1:
+                att_grouped = work.tile([P, P, 4], BF16, tag="att_grouped", align_bytes=64)
+                nc.vector.tensor_copy(out=att_grouped[:], in_=att_t[:].rearrange("p t b -> p b t"))
+                nc.vector.quantize_mx(
+                    out=att_codes[:, g, :].bitcast(FP8X4),
+                    scales=att_planes[:, g, :],
+                    in_=att_grouped[:].rearrange("p b t -> p (b t)"),
+                )
+
+        for part in range(H // N_BLOCK):
+            cols = slice(part * N_BLOCK, (part + 1) * N_BLOCK)
+            cell = work.tile([P, 8, N_BLOCK], F32, tag="T")
+            for gate in range(4):
+                nb = gate * (H // N_BLOCK) + part
+                acc = psum.tile([P, N_BLOCK], F32, tag="acc")
+                for g in range(H_PASSES):
+                    nc.tensor.matmul_mx(
+                        out=acc[:],
+                        lhsT=att_codes[:, g, :].bitcast(FP8X4),
+                        lhsT_scale=att_planes[:, g, :],
+                        rhs=wa_codes[:, nb, g, :].bitcast(FP8X4),
+                        rhs_scale=wa_planes[:, nb, g, :],
+                        start=(g == 0),
+                        stop=(g == H_PASSES - 1),
+                    )
+                nc.vector.tensor_tensor(
+                    out=cell[:, gate, :], in0=acc[:], in1=gates_xh[:, nb * N_BLOCK : (nb + 1) * N_BLOCK], op=ALU.add
+                )
+                nc.scalar.activation(
+                    out=cell[:, gate, :], in_=cell[:, gate, :], func=(ACT.Tanh if gate == 2 else ACT.Sigmoid)
+                )
+            gate_i, gate_f, gate_g, gate_o = [cell[:, gate, :] for gate in range(4)]
+            kept, c_new, tanh_c, h_new = [cell[:, 4 + i, :] for i in range(4)]
+            nc.vector.tensor_tensor(out=kept, in0=gate_f, in1=c_sb[:, cols], op=ALU.mult)
+            nc.vector.tensor_tensor(out=c_new, in0=gate_i, in1=gate_g, op=ALU.mult)
+            nc.vector.tensor_tensor(out=c_new, in0=c_new, in1=kept, op=ALU.add)
+            nc.sync.dma_start(out=out_1[:, cols], in_=c_new)
+            nc.scalar.activation(out=tanh_c, in_=c_new, func=ACT.Tanh)
+            nc.vector.tensor_tensor(out=h_new, in0=gate_o, in1=tanh_c, op=ALU.mult)
+            nc.sync.dma_start(out=out_0[:, cols], in_=h_new)

@@ -20,18 +20,28 @@ PASS_WORDS = K_PASS // 2
 H_PASSES = H // K_PASS
 N_BLOCK = 512
 ROW_TILES = N_BLOCK // P
-GATE_BLOCKS = 4 * H // N_BLOCK
+H_BLOCKS = H // N_BLOCK
+GATE_BLOCKS = 4 * H_BLOCKS
 GROUP = 256
 GROUPS = H // GROUP
+CHUNKS = 2 * GROUPS
+QUARTER = S // 4
+S_HALF = S // 2
 
 FLOPS = 2 * P * (H * H + 4 * H * 3 * H)
 
 
-def quantise_weight_pass(nc, psum, stage, ident, words, codes, plane):
+def load_weight_rows(nc, stage, rows):
+    w_rows = stage.tile([P, ROW_TILES, H], BF16, tag="w_rows", bufs=4)
+    nc.sync.dma_start(out=w_rows[:], in_=rows.rearrange("(t p) k -> p t k", p=P))
+    return w_rows[:].bitcast(F32)
+
+
+def quantise_weight_pass(nc, psum, stage, ident, words, codes, plane, vector_helps):
     grouped = stage.tile([P, 4 * N_BLOCK], BF16, tag="grouped", bufs=3, align_bytes=64)
     grouped_words = grouped[:].bitcast(F32).rearrange("p (r u) -> p r u", u=2)
     for pair in range(ROW_TILES // 2):
-        bank = psum.tile([P, 2, 2 * P], F32, tag="wt", bufs=4)
+        bank = psum.tile([P, 2, 2 * P], F32, tag="wt", bufs=3)
         for i in range(2):
             for u in range(2):
                 nc.tensor.transpose(
@@ -39,19 +49,20 @@ def quantise_weight_pass(nc, psum, stage, ident, words, codes, plane):
                     words[:, 2 * pair + i, u * P : (u + 1) * P],
                     ident[:],
                 )
-        nc.scalar.copy(
-            out=grouped_words[:, pair * 2 * P : (pair + 1) * 2 * P, :],
-            in_=bank[:].rearrange("p u r -> p r u"),
-        )
+        rows = slice(pair * 2 * P, (pair + 1) * 2 * P)
+        if vector_helps and pair == 1:
+            nc.vector.tensor_copy(out=grouped_words[:, rows, :], in_=bank[:].rearrange("p u r -> p r u"))
+        else:
+            nc.scalar.copy(out=grouped_words[:, rows, :], in_=bank[:].rearrange("p u r -> p r u"))
     nc.vector.quantize_mx(out=codes.bitcast(FP8X4), scales=plane, in_=grouped[:])
 
 
 def quantise_activations(nc, psum, stage, ident, rows, codes, planes):
     words = rows[:].bitcast(F32)
-    bank = psum.tile([P, 2 * H_PASSES, P], F32, tag="wt", bufs=4)
+    bank = psum.tile([P, 2 * H_PASSES, P], F32, tag="wt", bufs=3)
     for q in range(2 * H_PASSES):
         nc.tensor.transpose(bank[:, q, :], words[:, q * P : (q + 1) * P], ident[:])
-    grouped = stage.tile([P, 4 * H_PASSES * P], BF16, tag="act_grouped", bufs=2, align_bytes=64)
+    grouped = stage.tile([P, 4 * H_PASSES * P], BF16, tag="act_grouped", bufs=1, align_bytes=64)
     nc.scalar.copy(
         out=grouped[:].bitcast(F32).rearrange("p (g b u) -> p g b u", g=H_PASSES, u=2),
         in_=bank[:].rearrange("p (g u) b -> p g b u", u=2),
@@ -61,6 +72,27 @@ def quantise_activations(nc, psum, stage, ident, rows, codes, planes):
         scales=planes[:].rearrange("p g b -> p (g b)"),
         in_=grouped[:],
     )
+
+
+def multiply_passes(nc, psum, stage, ident, acc, operands):
+    for i, (w_words, act_codes, act_planes) in enumerate(operands):
+        for g in range(H_PASSES):
+            w_codes = stage.tile([P, N_BLOCK], U32, tag="w_codes", bufs=4, align_bytes=64)
+            w_plane = stage.tile([P, N_BLOCK], U8, tag="w_plane", bufs=4, align_bytes=64)
+            quantise_weight_pass(
+                nc, psum, stage, ident,
+                w_words[:, :, g * PASS_WORDS : (g + 1) * PASS_WORDS], w_codes[:], w_plane[:],
+                vector_helps=(g == 1),
+            )
+            nc.tensor.matmul_mx(
+                out=acc[:],
+                lhsT=act_codes[:, g, :].bitcast(FP8X4),
+                lhsT_scale=act_planes[:, g, :],
+                rhs=w_codes[:].bitcast(FP8X4),
+                rhs_scale=w_plane[:],
+                start=(i == 0 and g == 0),
+                stop=(i == len(operands) - 1 and g == H_PASSES - 1),
+            )
 
 
 def tile_decoderlstm_pa_kernel(
@@ -74,46 +106,34 @@ def tile_decoderlstm_pa_kernel(
         work = stack.enter_context(tc.tile_pool(name="work", bufs=2))
         psum = stack.enter_context(tc.psum_pool(name="psum", bufs=2))
 
+        def load_enc_group(group):
+            enc = work.tile([P, S, GROUP], BF16, tag="enc")
+            feats = slice(group * GROUP, (group + 1) * GROUP)
+            for i in range(S // QUARTER):
+                steps = slice(i * QUARTER, (i + 1) * QUARTER)
+                nc.sync.dma_start(out=enc[:, steps, :], in_=enc_seq[steps, :, feats].rearrange("s b j -> b s j"))
+            return enc
+
         ident = const.tile([P, P], F32)
         make_identity(nc, ident[:])
         ones = const.tile([P, P], BF16)
         nc.vector.memset(ones[:], 1.0)
 
-        x_sb = keep.tile([P, H], BF16)
+        enc_groups = [load_enc_group(0)]
+        x_sb = stage.tile([P, H], BF16, tag="w_rows", bufs=4)
         nc.sync.dma_start(out=x_sb[:], in_=x)
-        bias_rows = work.tile([P, 5 * H], BF16, tag="T")
+        attn_w_words = [
+            load_weight_rows(nc, stage, attn_W[nb * N_BLOCK : (nb + 1) * N_BLOCK, :]) for nb in range(H_BLOCKS)
+        ]
+        bias_rows = work.tile([P, 5 * H], BF16, tag="exps")
         nc.vector.memset(bias_rows[:].bitcast(I32), 0)
         nc.sync.dma_start(out=bias_rows[0:1, 4 * H : 5 * H], in_=attn_b.rearrange("(o n) -> o n", o=1))
-        attn_w = stage.tile([P, 2 * ROW_TILES, H], BF16, tag="wih")
-        attn_w_rows = attn_W.rearrange("(t p) k -> p t k", p=P)
-        for nb in range(H // N_BLOCK):
-            tiles = slice(nb * ROW_TILES, (nb + 1) * ROW_TILES)
-            nc.sync.dma_start(out=attn_w[:, tiles, :], in_=attn_w_rows[:, tiles, :])
         nc.sync.dma_start(out=bias_rows[0:1, 0 : 4 * H], in_=b_ih0.rearrange("(o n) -> o n", o=1))
         nc.sync.dma_start(out=bias_rows[1:2, 0 : 4 * H], in_=b_hh0.rearrange("(o n) -> o n", o=1))
-        h_sb = keep.tile([P, H], BF16)
+        h_sb = stage.tile([P, H], BF16, tag="w_rows", bufs=4)
         nc.sync.dma_start(out=h_sb[:], in_=h_prev)
         c_sb = keep.tile([P, H], BF16)
         nc.sync.dma_start(out=c_sb[:], in_=c_prev)
-
-        attn_lin = keep.tile([P, H], F32)
-        gates_xh = keep.tile([P, 4 * H], F32)
-        for nb in range(H // N_BLOCK):
-            cols = slice(nb * N_BLOCK, (nb + 1) * N_BLOCK)
-            spread = psum.tile([P, N_BLOCK], F32, tag="acc")
-            nc.tensor.matmul(
-                out=spread[:],
-                lhsT=ones[:],
-                rhs=bias_rows[:, 4 * H + nb * N_BLOCK : 4 * H + (nb + 1) * N_BLOCK],
-                start=True,
-                stop=True,
-            )
-            nc.scalar.copy(out=attn_lin[:, cols], in_=spread[:])
-        for nb in range(GATE_BLOCKS):
-            cols = slice(nb * N_BLOCK, (nb + 1) * N_BLOCK)
-            spread = psum.tile([P, N_BLOCK], F32, tag="acc")
-            nc.tensor.matmul(out=spread[:], lhsT=ones[:], rhs=bias_rows[:, cols], start=True, stop=True)
-            nc.scalar.copy(out=gates_xh[:, cols], in_=spread[:])
 
         x_codes = keep.tile([P, H_PASSES, P], U32, align_bytes=64)
         x_planes = keep.tile([P, H_PASSES, P], U8, align_bytes=64)
@@ -122,28 +142,25 @@ def tile_decoderlstm_pa_kernel(
         h_planes = keep.tile([P, H_PASSES, P], U8, align_bytes=64)
         quantise_activations(nc, psum, stage, ident, h_sb, h_codes, h_planes)
 
-        attn_w_words = attn_w[:].bitcast(F32)
-        for nb in range(H // N_BLOCK):
+        attn_lin = keep.tile([P, H], F32)
+        for nb in range(H_BLOCKS):
             cols = slice(nb * N_BLOCK, (nb + 1) * N_BLOCK)
+            spread = psum.tile([P, N_BLOCK], F32, tag="acc")
+            nc.tensor.matmul(
+                out=spread[:], lhsT=ones[:], rhs=bias_rows[:, 4 * H + nb * N_BLOCK : 4 * H + (nb + 1) * N_BLOCK],
+                start=True, stop=True,
+            )
+            nc.scalar.copy(out=attn_lin[:, cols], in_=spread[:])
             acc = psum.tile([P, N_BLOCK], F32, tag="acc")
-            for g in range(H_PASSES):
-                w_codes = stage.tile([P, N_BLOCK], U32, tag="w_codes", bufs=4, align_bytes=64)
-                w_plane = stage.tile([P, N_BLOCK], U8, tag="w_plane", bufs=4, align_bytes=64)
-                quantise_weight_pass(
-                    nc, psum, stage, ident,
-                    attn_w_words[:, nb * ROW_TILES : (nb + 1) * ROW_TILES, g * PASS_WORDS : (g + 1) * PASS_WORDS],
-                    w_codes[:], w_plane[:],
-                )
-                nc.tensor.matmul_mx(
-                    out=acc[:],
-                    lhsT=x_codes[:, g, :].bitcast(FP8X4),
-                    lhsT_scale=x_planes[:, g, :],
-                    rhs=w_codes[:].bitcast(FP8X4),
-                    rhs_scale=w_plane[:],
-                    start=(g == 0),
-                    stop=(g == H_PASSES - 1),
-                )
+            multiply_passes(nc, psum, stage, ident, acc, [(attn_w_words[nb], x_codes, x_planes)])
             nc.vector.tensor_tensor(out=attn_lin[:, cols], in0=acc[:], in1=attn_lin[:, cols], op=ALU.add)
+
+        gates_xh = keep.tile([P, 4 * H], F32)
+        for nb in range(GATE_BLOCKS):
+            cols = slice(nb * N_BLOCK, (nb + 1) * N_BLOCK)
+            spread = psum.tile([P, N_BLOCK], F32, tag="acc")
+            nc.tensor.matmul(out=spread[:], lhsT=ones[:], rhs=bias_rows[:, cols], start=True, stop=True)
+            nc.scalar.copy(out=gates_xh[:, cols], in_=spread[:])
 
         wa_codes = keep.tile([P, GATE_BLOCKS, H_PASSES, N_BLOCK], U32, align_bytes=64)
         wa_planes = keep.tile([P, GATE_BLOCKS, H_PASSES, N_BLOCK], U8, align_bytes=64)
@@ -152,99 +169,107 @@ def tile_decoderlstm_pa_kernel(
 
         def gate_block(nb):
             rows = slice(nb * N_BLOCK, (nb + 1) * N_BLOCK)
-            w_ih = stage.tile([P, ROW_TILES, 2 * H], BF16, tag="wih")
-            nc.sync.dma_start(out=w_ih[:], in_=W_ih0[rows, :].rearrange("(t p) k -> p t k", p=P))
-            w_hh = stage.tile([P, ROW_TILES, H], BF16, tag="whh")
-            nc.sync.dma_start(out=w_hh[:], in_=W_hh0[rows, :].rearrange("(t p) k -> p t k", p=P))
-            w_ih_words = w_ih[:].bitcast(F32)
-            w_hh_words = w_hh[:].bitcast(F32)
+            wx_words = load_weight_rows(nc, stage, W_ih0[rows, 0:H])
+            wh_words = load_weight_rows(nc, stage, W_hh0[rows, :])
+            wa_words = load_weight_rows(nc, stage, W_ih0[rows, H : 2 * H])
             acc = psum.tile([P, N_BLOCK], F32, tag="acc")
-            sources = ((w_ih_words, x_codes, x_planes), (w_hh_words, h_codes, h_planes))
-            for i, (w_words, act_codes, act_planes) in enumerate(sources):
-                for g in range(H_PASSES):
-                    w_codes = stage.tile([P, N_BLOCK], U32, tag="w_codes", bufs=4, align_bytes=64)
-                    w_plane = stage.tile([P, N_BLOCK], U8, tag="w_plane", bufs=4, align_bytes=64)
-                    quantise_weight_pass(
-                        nc, psum, stage, ident,
-                        w_words[:, :, g * PASS_WORDS : (g + 1) * PASS_WORDS],
-                        w_codes[:], w_plane[:],
-                    )
-                    nc.tensor.matmul_mx(
-                        out=acc[:],
-                        lhsT=act_codes[:, g, :].bitcast(FP8X4),
-                        lhsT_scale=act_planes[:, g, :],
-                        rhs=w_codes[:].bitcast(FP8X4),
-                        rhs_scale=w_plane[:],
-                        start=(i == 0 and g == 0),
-                        stop=(i == 1 and g == H_PASSES - 1),
-                    )
+            multiply_passes(
+                nc, psum, stage, ident, acc, [(wx_words, x_codes, x_planes), (wh_words, h_codes, h_planes)]
+            )
             nc.vector.tensor_tensor(out=gates_xh[:, rows], in0=acc[:], in1=gates_xh[:, rows], op=ALU.add)
             for g in range(H_PASSES):
                 quantise_weight_pass(
                     nc, psum, stage, ident,
-                    w_ih_words[:, :, (H_PASSES + g) * PASS_WORDS : (H_PASSES + g + 1) * PASS_WORDS],
+                    wa_words[:, :, g * PASS_WORDS : (g + 1) * PASS_WORDS],
                     wa_codes[:, nb, g, :], wa_planes[:, nb, g, :],
+                    vector_helps=(g == 1),
                 )
 
-        for group in range(GROUPS):
+        def negated_peaks(group):
+            enc = enc_groups[group]
             feats = slice(group * GROUP, (group + 1) * GROUP)
-            enc = work.tile([P, S, GROUP], BF16, tag="enc")
-            nc.sync.dma_start(out=enc[:], in_=enc_seq[:, :, feats].rearrange("s b j -> b s j"))
-
-            top = work.tile([P, S // 4, GROUP], BF16, tag="top", bufs=1)
-            low = work.tile([P, S // 4, GROUP], BF16, tag="low", bufs=1)
-            quarter = S // 4
-            nc.vector.tensor_tensor(out=top[:], in0=enc[:, 0:quarter, :], in1=enc[:, quarter : 2 * quarter, :], op=ALU.max)
-            nc.vector.tensor_tensor(out=low[:], in0=enc[:, 0:quarter, :], in1=enc[:, quarter : 2 * quarter, :], op=ALU.min)
-            for i in range(2, 4):
-                nc.vector.tensor_tensor(out=top[:], in0=top[:], in1=enc[:, i * quarter : (i + 1) * quarter, :], op=ALU.max)
-                nc.vector.tensor_tensor(out=low[:], in0=low[:], in1=enc[:, i * quarter : (i + 1) * quarter, :], op=ALU.min)
-            half = quarter // 2
+            top = work.tile([P, QUARTER, GROUP], BF16, tag="top", bufs=1)
+            low = work.tile([P, QUARTER, GROUP], BF16, tag="low", bufs=1)
+            nc.vector.tensor_tensor(out=top[:], in0=enc[:, 0:QUARTER, :], in1=enc[:, QUARTER : 2 * QUARTER, :], op=ALU.max)
+            nc.vector.tensor_tensor(out=low[:], in0=enc[:, 0:QUARTER, :], in1=enc[:, QUARTER : 2 * QUARTER, :], op=ALU.min)
+            for i in range(2, S // QUARTER):
+                steps = slice(i * QUARTER, (i + 1) * QUARTER)
+                nc.vector.tensor_tensor(out=top[:], in0=top[:], in1=enc[:, steps, :], op=ALU.max)
+                nc.vector.tensor_tensor(out=low[:], in0=low[:], in1=enc[:, steps, :], op=ALU.min)
+            half = QUARTER // 2
             while half >= 1:
                 nc.vector.tensor_tensor(out=top[:, 0:half, :], in0=top[:, 0:half, :], in1=top[:, half : 2 * half, :], op=ALU.max)
                 nc.vector.tensor_tensor(out=low[:, 0:half, :], in0=low[:, 0:half, :], in1=low[:, half : 2 * half, :], op=ALU.min)
                 half //= 2
-            at_top = work.tile([P, GROUP], F32, tag="at_top")
-            at_low = work.tile([P, GROUP], F32, tag="at_low")
-            peak = work.tile([P, GROUP], F32, tag="peak")
-            nc.vector.tensor_tensor(out=at_top[:], in0=attn_lin[:, feats], in1=top[:, 0, :], op=ALU.mult)
-            nc.vector.tensor_tensor(out=at_low[:], in0=attn_lin[:, feats], in1=low[:, 0, :], op=ALU.mult)
-            nc.vector.tensor_tensor(out=peak[:], in0=at_top[:], in1=at_low[:], op=ALU.max)
+            neg_top = work.tile([P, GROUP], F32, tag="neg_top", bufs=1)
+            neg_low = work.tile([P, GROUP], F32, tag="neg_low", bufs=1)
+            neg_peak = work.tile([P, GROUP], F32, tag="neg_peak")
+            nc.vector.scalar_tensor_tensor(
+                out=neg_top[:], in0=attn_lin[:, feats], scalar=-1.0, in1=top[:, 0, :], op0=ALU.mult, op1=ALU.mult
+            )
+            nc.vector.scalar_tensor_tensor(
+                out=neg_low[:], in0=attn_lin[:, feats], scalar=-1.0, in1=low[:, 0, :], op0=ALU.mult, op1=ALU.mult
+            )
+            nc.vector.tensor_tensor(out=neg_peak[:], in0=neg_top[:], in1=neg_low[:], op=ALU.min)
+            return neg_peak
 
+        def exponentials(chunk, neg_peak):
+            group, e = divmod(chunk, 2)
+            enc = enc_groups[group]
+            exps = work.tile([P, P, S], F32, tag="exps")
+            exp_sum = work.tile([P, P], F32, tag="exp_sum")
+            for p in range(P):
+                j = 2 * p + e
+                nc.scalar.activation(
+                    out=exps[:, p, :],
+                    in_=enc[:, :, j],
+                    func=ACT.Exp,
+                    scale=attn_lin[:, group * GROUP + j : group * GROUP + j + 1],
+                    bias=neg_peak[:, j : j + 1],
+                    accum_out=exp_sum[:, p : p + 1],
+                )
+            return exps, exp_sum
+
+        def weighted_mean(chunk, exps, exp_sum, mean):
+            group, e = divmod(chunk, 2)
+            enc_c = enc_groups[group][:].rearrange("b s (p e) -> b s e p", e=2)[:, :, e, :]
+            exp_sum_t = psum.tile([P, P], F32, tag="sums", bufs=3)
+            nc.tensor.transpose(exp_sum_t[:], exp_sum[:], ident[:])
+            inverse = work.tile([P, P], F32, tag="inverse")
+            nc.vector.reciprocal(out=inverse[:], in_=exp_sum_t[:])
+            total = psum.tile([P, P], F32, tag="sums", bufs=3)
+            for part in range(S // S_HALF):
+                steps = slice(part * S_HALF, (part + 1) * S_HALF)
+                terms = work.tile([P, S_HALF, P], F32, tag="terms", bufs=3)
+                nc.vector.tensor_tensor(
+                    out=terms[:], in0=exps[:].rearrange("b p s -> b s p")[:, steps, :], in1=enc_c[:, steps, :], op=ALU.mult
+                )
+                for i in range(S_HALF):
+                    s = part * S_HALF + i
+                    nc.tensor.matmul(
+                        out=total[:], lhsT=terms[:, i, :], rhs=ident[:], is_transpose=True,
+                        start=(s == 0), stop=(s == S - 1),
+                    )
+            nc.vector.tensor_tensor(out=mean, in0=total[:], in1=inverse[:], op=ALU.mult)
+            return inverse
+
+        neg_peak = negated_peaks(0)
+        ready = exponentials(0, neg_peak)
+        for chunk in range(CHUNKS):
+            group, e = divmod(chunk, 2)
             g, u = divmod(group, 2)
-            if u == 0:
+            exps, exp_sum = ready
+            if e == 0 and group + 1 < GROUPS:
+                enc_groups.append(load_enc_group(group + 1))
+            gate_block(chunk)
+            if chunk + 1 < CHUNKS:
+                if e == 1:
+                    neg_peak = negated_peaks(group + 1)
+                ready = exponentials(chunk + 1, neg_peak)
+            if e == 0 and u == 0:
                 att_t = work.tile([P, 4, P], F32, tag="att_t")
-            for e in range(2):
-                enc_c = enc[:].rearrange("b s (p e) -> b s e p", e=2)[:, :, e, :]
-                lin_c = attn_lin[:, feats].rearrange("b (p e) -> b e p", e=2)[:, e, :]
-                peak_c = peak[:].rearrange("b (p e) -> b e p", e=2)[:, e, :]
-                terms = work.tile([P, S, P], F32, tag="T")
-                nc.vector.tensor_tensor(
-                    out=terms[:], in0=enc_c, in1=lin_c.unsqueeze(1).to_broadcast([P, S, P]), op=ALU.mult
-                )
-                nc.vector.tensor_tensor(
-                    out=terms[:], in0=terms[:], in1=peak_c.unsqueeze(1).to_broadcast([P, S, P]), op=ALU.subtract
-                )
-                nc.scalar.activation(out=terms[:], in_=terms[:], func=ACT.Exp)
-                sums = psum.tile([P, 2, P], F32, tag="sums")
-                for s in range(S):
-                    nc.tensor.matmul(
-                        out=sums[:, 0, :], lhsT=terms[:, s, :], rhs=ident[:], is_transpose=True,
-                        start=(s == 0), stop=(s == S - 1),
-                    )
-                nc.vector.tensor_tensor(out=terms[:], in0=terms[:], in1=enc_c, op=ALU.mult)
-                for s in range(S):
-                    nc.tensor.matmul(
-                        out=sums[:, 1, :], lhsT=terms[:, s, :], rhs=ident[:], is_transpose=True,
-                        start=(s == 0), stop=(s == S - 1),
-                    )
-                inverse = work.tile([P, P], F32, tag="inverse")
-                nc.vector.reciprocal(out=inverse[:], in_=sums[:, 0, :])
-                nc.vector.tensor_tensor(out=att_t[:, 2 * u + e, :], in0=sums[:, 1, :], in1=inverse[:], op=ALU.mult)
-
-                gate_block(2 * group + e)
-
-            if u == 1:
+            inverse = weighted_mean(chunk, exps, exp_sum, att_t[:, 2 * u + e, :])
+            if e == 1 and u == 1:
                 att_grouped = work.tile([P, P, 4], BF16, tag="att_grouped", align_bytes=64)
                 nc.vector.tensor_copy(out=att_grouped[:], in_=att_t[:].rearrange("p t b -> p b t"))
                 nc.vector.quantize_mx(
@@ -253,11 +278,14 @@ def tile_decoderlstm_pa_kernel(
                     in_=att_grouped[:].rearrange("p b t -> p (b t)"),
                 )
 
-        for part in range(H // N_BLOCK):
+        warm = work.tile([P, 1], F32, tag="warm", bufs=1)
+        nc.scalar.activation(out=warm[:], in_=inverse[:, 0:1], func=ACT.Sigmoid)
+
+        for part in range(H_BLOCKS):
             cols = slice(part * N_BLOCK, (part + 1) * N_BLOCK)
-            cell = work.tile([P, 8, N_BLOCK], F32, tag="T")
+            cell = work.tile([P, 8, N_BLOCK], F32, tag="exps")
             for gate in range(4):
-                nb = gate * (H // N_BLOCK) + part
+                nb = gate * H_BLOCKS + part
                 acc = psum.tile([P, N_BLOCK], F32, tag="acc")
                 for g in range(H_PASSES):
                     nc.tensor.matmul_mx(

@@ -32,7 +32,7 @@ FLOPS = 2 * P * (H * H + 4 * H * 3 * H)
 
 
 def load_weight_rows(nc, stage, rows):
-    w_rows = stage.tile([P, ROW_TILES, H], BF16, tag="w_rows", bufs=4)
+    w_rows = stage.tile([P, ROW_TILES, H], BF16, tag="w_rows", bufs=3)
     nc.sync.dma_start(out=w_rows[:], in_=rows.rearrange("(t p) k -> p t k", p=P))
     return w_rows[:].bitcast(F32)
 
@@ -120,7 +120,7 @@ def tile_decoderlstm_pa_kernel(
         nc.vector.memset(ones[:], 1.0)
 
         enc_groups = [load_enc_group(0)]
-        x_sb = stage.tile([P, H], BF16, tag="w_rows", bufs=4)
+        x_sb = stage.tile([P, H], BF16, tag="w_rows", bufs=3)
         nc.sync.dma_start(out=x_sb[:], in_=x)
         attn_w_words = [
             load_weight_rows(nc, stage, attn_W[nb * N_BLOCK : (nb + 1) * N_BLOCK, :]) for nb in range(H_BLOCKS)
@@ -130,7 +130,7 @@ def tile_decoderlstm_pa_kernel(
         nc.sync.dma_start(out=bias_rows[0:1, 4 * H : 5 * H], in_=attn_b.rearrange("(o n) -> o n", o=1))
         nc.sync.dma_start(out=bias_rows[0:1, 0 : 4 * H], in_=b_ih0.rearrange("(o n) -> o n", o=1))
         nc.sync.dma_start(out=bias_rows[1:2, 0 : 4 * H], in_=b_hh0.rearrange("(o n) -> o n", o=1))
-        h_sb = stage.tile([P, H], BF16, tag="w_rows", bufs=4)
+        h_sb = stage.tile([P, H], BF16, tag="w_rows", bufs=3)
         nc.sync.dma_start(out=h_sb[:], in_=h_prev)
         c_sb = keep.tile([P, H], BF16)
         nc.sync.dma_start(out=c_sb[:], in_=c_prev)
@@ -217,7 +217,6 @@ def tile_decoderlstm_pa_kernel(
             group, e = divmod(chunk, 2)
             enc = enc_groups[group]
             exps = work.tile([P, P, S], F32, tag="exps")
-            exp_sum = work.tile([P, P], F32, tag="exp_sum")
             for p in range(P):
                 j = 2 * p + e
                 nc.scalar.activation(
@@ -226,30 +225,32 @@ def tile_decoderlstm_pa_kernel(
                     func=ACT.Exp,
                     scale=attn_lin[:, group * GROUP + j : group * GROUP + j + 1],
                     bias=neg_peak[:, j : j + 1],
-                    accum_out=exp_sum[:, p : p + 1],
                 )
-            return exps, exp_sum
+            return exps
 
-        def weighted_mean(chunk, exps, exp_sum, mean):
+        def sum_over_s(total, terms, part):
+            for i in range(S_HALF):
+                s = part * S_HALF + i
+                nc.tensor.matmul(
+                    out=total[:], lhsT=terms[:, i, :], rhs=ident[:], is_transpose=True,
+                    start=(s == 0), stop=(s == S - 1),
+                )
+
+        def weighted_mean(chunk, exps, mean):
             group, e = divmod(chunk, 2)
             enc_c = enc_groups[group][:].rearrange("b s (p e) -> b s e p", e=2)[:, :, e, :]
-            exp_sum_t = psum.tile([P, P], F32, tag="sums", bufs=3)
-            nc.tensor.transpose(exp_sum_t[:], exp_sum[:], ident[:])
-            inverse = work.tile([P, P], F32, tag="inverse")
-            nc.vector.reciprocal(out=inverse[:], in_=exp_sum_t[:])
+            exp_total = psum.tile([P, P], F32, tag="sums", bufs=3)
             total = psum.tile([P, P], F32, tag="sums", bufs=3)
             for part in range(S // S_HALF):
                 steps = slice(part * S_HALF, (part + 1) * S_HALF)
-                terms = work.tile([P, S_HALF, P], F32, tag="terms", bufs=3)
-                nc.vector.tensor_tensor(
-                    out=terms[:], in0=exps[:].rearrange("b p s -> b s p")[:, steps, :], in1=enc_c[:, steps, :], op=ALU.mult
-                )
-                for i in range(S_HALF):
-                    s = part * S_HALF + i
-                    nc.tensor.matmul(
-                        out=total[:], lhsT=terms[:, i, :], rhs=ident[:], is_transpose=True,
-                        start=(s == 0), stop=(s == S - 1),
-                    )
+                turned = work.tile([P, S_HALF, P], F32, tag="terms", bufs=4)
+                nc.vector.tensor_copy(out=turned[:], in_=exps[:].rearrange("b p s -> b s p")[:, steps, :])
+                sum_over_s(exp_total, turned, part)
+                terms = work.tile([P, S_HALF, P], F32, tag="terms", bufs=4)
+                nc.vector.tensor_tensor(out=terms[:], in0=turned[:], in1=enc_c[:, steps, :], op=ALU.mult)
+                sum_over_s(total, terms, part)
+            inverse = work.tile([P, P], F32, tag="inverse")
+            nc.vector.reciprocal(out=inverse[:], in_=exp_total[:])
             nc.vector.tensor_tensor(out=mean, in0=total[:], in1=inverse[:], op=ALU.mult)
             return inverse
 
@@ -258,7 +259,7 @@ def tile_decoderlstm_pa_kernel(
         for chunk in range(CHUNKS):
             group, e = divmod(chunk, 2)
             g, u = divmod(group, 2)
-            exps, exp_sum = ready
+            exps = ready
             if e == 0 and group + 1 < GROUPS:
                 enc_groups.append(load_enc_group(group + 1))
             gate_block(chunk)
@@ -268,7 +269,7 @@ def tile_decoderlstm_pa_kernel(
                 ready = exponentials(chunk + 1, neg_peak)
             if e == 0 and u == 0:
                 att_t = work.tile([P, 4, P], F32, tag="att_t")
-            inverse = weighted_mean(chunk, exps, exp_sum, att_t[:, 2 * u + e, :])
+            inverse = weighted_mean(chunk, exps, att_t[:, 2 * u + e, :])
             if e == 1 and u == 1:
                 att_grouped = work.tile([P, P, 4], BF16, tag="att_grouped", align_bytes=64)
                 nc.vector.tensor_copy(out=att_grouped[:], in_=att_t[:].rearrange("p t b -> p b t"))

@@ -24,20 +24,20 @@ H_BLOCKS = H // N_BLOCK
 GATE_BLOCKS = 4 * H_BLOCKS
 GROUP = 256
 GROUPS = H // GROUP
-CHUNKS = 2 * GROUPS
 QUARTER = S // 4
 S_HALF = S // 2
+HALVES = S // S_HALF
 
 FLOPS = 2 * P * (H * H + 4 * H * 3 * H)
 
 
 def load_weight_rows(nc, stage, rows):
-    w_rows = stage.tile([P, ROW_TILES, H], BF16, tag="w_rows", bufs=3)
+    w_rows = stage.tile([P, ROW_TILES, H], BF16, tag="w_rows", bufs=4)
     nc.sync.dma_start(out=w_rows[:], in_=rows.rearrange("(t p) k -> p t k", p=P))
     return w_rows[:].bitcast(F32)
 
 
-def quantise_weight_pass(nc, psum, stage, ident, words, codes, plane, vector_helps):
+def quantise_weight_pass(nc, psum, stage, ident, words, codes, plane):
     grouped = stage.tile([P, 4 * N_BLOCK], BF16, tag="grouped", bufs=3, align_bytes=64)
     grouped_words = grouped[:].bitcast(F32).rearrange("p (r u) -> p r u", u=2)
     for pair in range(ROW_TILES // 2):
@@ -49,11 +49,10 @@ def quantise_weight_pass(nc, psum, stage, ident, words, codes, plane, vector_hel
                     words[:, 2 * pair + i, u * P : (u + 1) * P],
                     ident[:],
                 )
-        rows = slice(pair * 2 * P, (pair + 1) * 2 * P)
-        if vector_helps and pair == 1:
-            nc.vector.tensor_copy(out=grouped_words[:, rows, :], in_=bank[:].rearrange("p u r -> p r u"))
-        else:
-            nc.scalar.copy(out=grouped_words[:, rows, :], in_=bank[:].rearrange("p u r -> p r u"))
+        nc.scalar.copy(
+            out=grouped_words[:, pair * 2 * P : (pair + 1) * 2 * P, :],
+            in_=bank[:].rearrange("p u r -> p r u"),
+        )
     nc.vector.quantize_mx(out=codes.bitcast(FP8X4), scales=plane, in_=grouped[:])
 
 
@@ -75,24 +74,26 @@ def quantise_activations(nc, psum, stage, ident, rows, codes, planes):
 
 
 def multiply_passes(nc, psum, stage, ident, acc, operands):
-    for i, (w_words, act_codes, act_planes) in enumerate(operands):
+    passes = []
+    for w_words, act_codes, act_planes in operands:
         for g in range(H_PASSES):
             w_codes = stage.tile([P, N_BLOCK], U32, tag="w_codes", bufs=4, align_bytes=64)
             w_plane = stage.tile([P, N_BLOCK], U8, tag="w_plane", bufs=4, align_bytes=64)
             quantise_weight_pass(
                 nc, psum, stage, ident,
                 w_words[:, :, g * PASS_WORDS : (g + 1) * PASS_WORDS], w_codes[:], w_plane[:],
-                vector_helps=(g == 1),
             )
-            nc.tensor.matmul_mx(
-                out=acc[:],
-                lhsT=act_codes[:, g, :].bitcast(FP8X4),
-                lhsT_scale=act_planes[:, g, :],
-                rhs=w_codes[:].bitcast(FP8X4),
-                rhs_scale=w_plane[:],
-                start=(i == 0 and g == 0),
-                stop=(i == len(operands) - 1 and g == H_PASSES - 1),
-            )
+            passes.append((act_codes[:, g, :], act_planes[:, g, :], w_codes, w_plane))
+    for i, (a_codes, a_plane, w_codes, w_plane) in enumerate(passes):
+        nc.tensor.matmul_mx(
+            out=acc[:],
+            lhsT=a_codes.bitcast(FP8X4),
+            lhsT_scale=a_plane,
+            rhs=w_codes[:].bitcast(FP8X4),
+            rhs_scale=w_plane[:],
+            start=(i == 0),
+            stop=(i == len(passes) - 1),
+        )
 
 
 def tile_decoderlstm_pa_kernel(
@@ -120,7 +121,7 @@ def tile_decoderlstm_pa_kernel(
         nc.vector.memset(ones[:], 1.0)
 
         enc_groups = [load_enc_group(0)]
-        x_sb = stage.tile([P, H], BF16, tag="w_rows", bufs=3)
+        x_sb = stage.tile([P, H], BF16, tag="w_rows", bufs=4)
         nc.sync.dma_start(out=x_sb[:], in_=x)
         attn_w_words = [
             load_weight_rows(nc, stage, attn_W[nb * N_BLOCK : (nb + 1) * N_BLOCK, :]) for nb in range(H_BLOCKS)
@@ -130,7 +131,7 @@ def tile_decoderlstm_pa_kernel(
         nc.sync.dma_start(out=bias_rows[0:1, 4 * H : 5 * H], in_=attn_b.rearrange("(o n) -> o n", o=1))
         nc.sync.dma_start(out=bias_rows[0:1, 0 : 4 * H], in_=b_ih0.rearrange("(o n) -> o n", o=1))
         nc.sync.dma_start(out=bias_rows[1:2, 0 : 4 * H], in_=b_hh0.rearrange("(o n) -> o n", o=1))
-        h_sb = stage.tile([P, H], BF16, tag="w_rows", bufs=3)
+        h_sb = stage.tile([P, H], BF16, tag="w_rows", bufs=4)
         nc.sync.dma_start(out=h_sb[:], in_=h_prev)
         c_sb = keep.tile([P, H], BF16)
         nc.sync.dma_start(out=c_sb[:], in_=c_prev)
@@ -182,7 +183,6 @@ def tile_decoderlstm_pa_kernel(
                     nc, psum, stage, ident,
                     wa_words[:, :, g * PASS_WORDS : (g + 1) * PASS_WORDS],
                     wa_codes[:, nb, g, :], wa_planes[:, nb, g, :],
-                    vector_helps=(g == 1),
                 )
 
         def negated_peaks(group):
@@ -213,64 +213,86 @@ def tile_decoderlstm_pa_kernel(
             nc.vector.tensor_tensor(out=neg_peak[:], in0=neg_top[:], in1=neg_low[:], op=ALU.min)
             return neg_peak
 
-        def exponentials(chunk, neg_peak):
-            group, e = divmod(chunk, 2)
+        def chunk_of(group, e):
+            return enc_groups[group][:].rearrange("b s (p e) -> b s e p", e=2)[:, :, e, :]
+
+        def sum_over_s(total, tiles, part):
+            for i in range(S_HALF):
+                s = part * S_HALF + i
+                nc.tensor.matmul(
+                    out=total[:], lhsT=tiles[:, i, :], rhs=ident[:], is_transpose=True,
+                    start=(s == 0), stop=(s == S - 1),
+                )
+
+        def exponentials_by_scalar(group, neg_peak):
             enc = enc_groups[group]
             exps = work.tile([P, P, S], F32, tag="exps")
+            exp_sum = work.tile([P, P], F32, tag="exp_sum")
             for p in range(P):
-                j = 2 * p + e
+                j = 2 * p + 1
                 nc.scalar.activation(
                     out=exps[:, p, :],
                     in_=enc[:, :, j],
                     func=ACT.Exp,
                     scale=attn_lin[:, group * GROUP + j : group * GROUP + j + 1],
                     bias=neg_peak[:, j : j + 1],
+                    accum_out=exp_sum[:, p : p + 1],
                 )
-            return exps
-
-        def sum_over_s(total, terms, part):
-            for i in range(S_HALF):
-                s = part * S_HALF + i
-                nc.tensor.matmul(
-                    out=total[:], lhsT=terms[:, i, :], rhs=ident[:], is_transpose=True,
-                    start=(s == 0), stop=(s == S - 1),
-                )
-
-        def weighted_mean(chunk, exps, mean):
-            group, e = divmod(chunk, 2)
-            enc_c = enc_groups[group][:].rearrange("b s (p e) -> b s e p", e=2)[:, :, e, :]
             exp_total = psum.tile([P, P], F32, tag="sums", bufs=3)
-            total = psum.tile([P, P], F32, tag="sums", bufs=3)
-            for part in range(S // S_HALF):
+            nc.tensor.transpose(exp_total[:], exp_sum[:], ident[:])
+            return exps[:].rearrange("b p s -> b s p"), exp_total
+
+        def exponentials_by_vector(group, e, neg_peak):
+            feats = slice(group * GROUP, (group + 1) * GROUP)
+            lin_c = attn_lin[:, feats].rearrange("b (p e) -> b e p", e=2)[:, e, :]
+            neg_peak_c = neg_peak[:].rearrange("b (p e) -> b e p", e=2)[:, e, :]
+            exps = work.tile([P, S, P], F32, tag="exps")
+            exp_total = psum.tile([P, P], F32, tag="sums", bufs=3)
+            for part in range(HALVES):
                 steps = slice(part * S_HALF, (part + 1) * S_HALF)
-                turned = work.tile([P, S_HALF, P], F32, tag="terms", bufs=4)
-                nc.vector.tensor_copy(out=turned[:], in_=exps[:].rearrange("b p s -> b s p")[:, steps, :])
-                sum_over_s(exp_total, turned, part)
-                terms = work.tile([P, S_HALF, P], F32, tag="terms", bufs=4)
-                nc.vector.tensor_tensor(out=terms[:], in0=turned[:], in1=enc_c[:, steps, :], op=ALU.mult)
-                sum_over_s(total, terms, part)
+                nc.vector.tensor_tensor(
+                    out=exps[:, steps, :], in0=chunk_of(group, e)[:, steps, :],
+                    in1=lin_c.unsqueeze(1).to_broadcast([P, S_HALF, P]), op=ALU.mult,
+                )
+                nc.vector.tensor_tensor(
+                    out=exps[:, steps, :], in0=exps[:, steps, :],
+                    in1=neg_peak_c.unsqueeze(1).to_broadcast([P, S_HALF, P]), op=ALU.add,
+                )
+                nc.scalar.activation(out=exps[:, steps, :], in_=exps[:, steps, :], func=ACT.Exp)
+                sum_over_s(exp_total, exps[:, steps, :], part)
+            return exps, exp_total
+
+        def weighted_mean(enc_c, exps_bsp, exp_total, mean):
             inverse = work.tile([P, P], F32, tag="inverse")
             nc.vector.reciprocal(out=inverse[:], in_=exp_total[:])
+            total = psum.tile([P, P], F32, tag="sums", bufs=3)
+            for part in range(HALVES):
+                steps = slice(part * S_HALF, (part + 1) * S_HALF)
+                terms = work.tile([P, S_HALF, P], F32, tag="terms", bufs=3)
+                nc.vector.tensor_tensor(out=terms[:], in0=exps_bsp[:, steps, :], in1=enc_c[:, steps, :], op=ALU.mult)
+                sum_over_s(total, terms, part)
             nc.vector.tensor_tensor(out=mean, in0=total[:], in1=inverse[:], op=ALU.mult)
             return inverse
 
         neg_peak = negated_peaks(0)
-        ready = exponentials(0, neg_peak)
-        for chunk in range(CHUNKS):
-            group, e = divmod(chunk, 2)
+        for group in range(GROUPS):
             g, u = divmod(group, 2)
-            exps = ready
-            if e == 0 and group + 1 < GROUPS:
-                enc_groups.append(load_enc_group(group + 1))
-            gate_block(chunk)
-            if chunk + 1 < CHUNKS:
-                if e == 1:
-                    neg_peak = negated_peaks(group + 1)
-                ready = exponentials(chunk + 1, neg_peak)
-            if e == 0 and u == 0:
+            if u == 0:
                 att_t = work.tile([P, 4, P], F32, tag="att_t")
-            inverse = weighted_mean(chunk, exps, att_t[:, 2 * u + e, :])
-            if e == 1 and u == 1:
+            gate_block(2 * group)
+            gate_block(2 * group + 1)
+
+            exps, exp_total = exponentials_by_vector(group, 0, neg_peak)
+            weighted_mean(chunk_of(group, 0), exps, exp_total, att_t[:, 2 * u, :])
+
+            if group + 1 < GROUPS:
+                enc_groups.append(load_enc_group(group + 1))
+                neg_peak_next = negated_peaks(group + 1)
+            exps, exp_total = exponentials_by_scalar(group, neg_peak)
+            inverse = weighted_mean(chunk_of(group, 1), exps, exp_total, att_t[:, 2 * u + 1, :])
+            neg_peak = neg_peak_next
+
+            if u == 1:
                 att_grouped = work.tile([P, P, 4], BF16, tag="att_grouped", align_bytes=64)
                 nc.vector.tensor_copy(out=att_grouped[:], in_=att_t[:].rearrange("p t b -> p b t"))
                 nc.vector.quantize_mx(

@@ -262,14 +262,22 @@ def tile_decoderlstm_pa_kernel(
                 sum_over_s(exp_total, exps[:, steps, :], part)
             return exps, exp_total
 
-        def weighted_mean(enc_c, exps_bsp, exp_total, mean):
+        def weighted_mean(enc_c, exps_bsp, exp_total, mean, s_is_innermost):
             inverse = work.tile([P, P], F32, tag="inverse")
             nc.vector.reciprocal(out=inverse[:], in_=exp_total[:])
             total = psum.tile([P, P], F32, tag="sums", bufs=3)
             for part in range(HALVES):
                 steps = slice(part * S_HALF, (part + 1) * S_HALF)
                 terms = work.tile([P, S_HALF, P], F32, tag="terms", bufs=3)
-                nc.vector.tensor_tensor(out=terms[:], in0=exps_bsp[:, steps, :], in1=enc_c[:, steps, :], op=ALU.mult)
+                if s_is_innermost:
+                    nc.vector.tensor_tensor(
+                        out=terms[:].rearrange("b (h l) p -> b h p l", l=2),
+                        in0=exps_bsp[:, steps, :].rearrange("b (h l) p -> b h p l", l=2),
+                        in1=enc_c[:, steps, :].rearrange("b (h l) p -> b h p l", l=2),
+                        op=ALU.mult,
+                    )
+                else:
+                    nc.vector.tensor_tensor(out=terms[:], in0=exps_bsp[:, steps, :], in1=enc_c[:, steps, :], op=ALU.mult)
                 sum_over_s(total, terms, part)
             nc.vector.tensor_tensor(out=mean, in0=total[:], in1=inverse[:], op=ALU.mult)
             return inverse
@@ -283,13 +291,13 @@ def tile_decoderlstm_pa_kernel(
             gate_block(2 * group + 1)
 
             exps, exp_total = exponentials_by_vector(group, 0, neg_peak)
-            weighted_mean(chunk_of(group, 0), exps, exp_total, att_t[:, 2 * u, :])
+            weighted_mean(chunk_of(group, 0), exps, exp_total, att_t[:, 2 * u, :], s_is_innermost=False)
 
             if group + 1 < GROUPS:
                 enc_groups.append(load_enc_group(group + 1))
                 neg_peak_next = negated_peaks(group + 1)
             exps, exp_total = exponentials_by_scalar(group, neg_peak)
-            inverse = weighted_mean(chunk_of(group, 1), exps, exp_total, att_t[:, 2 * u + 1, :])
+            inverse = weighted_mean(chunk_of(group, 1), exps, exp_total, att_t[:, 2 * u + 1, :], s_is_innermost=True)
             neg_peak = neg_peak_next
 
             if u == 1:

@@ -254,6 +254,8 @@ def tile_decoderlstm_pa_kernel(
                     out=exps[:, steps, :], in0=chunk_of(group, e)[:, steps, :],
                     in1=lin_c.unsqueeze(1).to_broadcast([P, S_HALF, P]), op=ALU.mult,
                 )
+            for part in range(HALVES):
+                steps = slice(part * S_HALF, (part + 1) * S_HALF)
                 nc.vector.tensor_tensor(
                     out=exps[:, steps, :], in0=exps[:, steps, :],
                     in1=neg_peak_c.unsqueeze(1).to_broadcast([P, S_HALF, P]), op=ALU.add,

from contextlib import ExitStack

import concourse.mybir as mybir
from concourse.masks import make_identity

F32 = mybir.dt.float32
BF16 = mybir.dt.bfloat16
I32 = mybir.dt.int32
U32 = mybir.dt.uint32
U8 = mybir.dt.uint8
FP8X4 = mybir.dt.float8_e4m3fn_x4
ALU = mybir.AluOpType
ACT = mybir.ActivationFunctionType

P = 128
H = 1024
S = 32
K_PASS = 512
PASS_WORDS = K_PASS // 2
H_PASSES = H // K_PASS
N_BLOCK = 512
ROW_TILES = N_BLOCK // P
H_BLOCKS = H // N_BLOCK
GATE_BLOCKS = 4 * H_BLOCKS
GROUP = 256
GROUPS = H // GROUP
QUARTER = S // 4
S_HALF = S // 2
HALVES = S // S_HALF

FLOPS = 2 * P * (H * H + 4 * H * 3 * H)


def load_weight_rows(nc, stage, rows):
    w_rows = stage.tile([P, ROW_TILES, H], BF16, tag="w_rows", bufs=4)
    nc.sync.dma_start(out=w_rows[:], in_=rows.rearrange("(t p) k -> p t k", p=P))
    return w_rows[:].bitcast(F32)


def quantise_weight_pass(nc, psum, stage, ident, words, codes, plane):
    grouped = stage.tile([P, 4 * N_BLOCK], BF16, tag="grouped", bufs=3, align_bytes=64)
    grouped_words = grouped[:].bitcast(F32).rearrange("p (r u) -> p r u", u=2)
    for pair in range(ROW_TILES // 2):
        bank = psum.tile([P, 2, 2 * P], F32, tag="wt", bufs=3)
        for i in range(2):
            for u in range(2):
                nc.tensor.transpose(
                    bank[:, u, i * P : (i + 1) * P],
                    words[:, 2 * pair + i, u * P : (u + 1) * P],
                    ident[:],
                )
        nc.scalar.copy(
            out=grouped_words[:, pair * 2 * P : (pair + 1) * 2 * P, :],
            in_=bank[:].rearrange("p u r -> p r u"),
        )
    nc.vector.quantize_mx(out=codes.bitcast(FP8X4), scales=plane, in_=grouped[:])


def quantise_activations(nc, psum, stage, ident, rows, codes, planes):
    words = rows[:].bitcast(F32)
    bank = psum.tile([P, 2 * H_PASSES, P], F32, tag="wt", bufs=3)
    for q in range(2 * H_PASSES):
        nc.tensor.transpose(bank[:, q, :], words[:, q * P : (q + 1) * P], ident[:])
    grouped = stage.tile([P, 4 * H_PASSES * P], BF16, tag="act_grouped", bufs=1, align_bytes=64)
    nc.scalar.copy(
        out=grouped[:].bitcast(F32).rearrange("p (g b u) -> p g b u", g=H_PASSES, u=2),
        in_=bank[:].rearrange("p (g u) b -> p g b u", u=2),
    )
    nc.vector.quantize_mx(
        out=codes[:].rearrange("p g b -> p (g b)").bitcast(FP8X4),
        scales=planes[:].rearrange("p g b -> p (g b)"),
        in_=grouped[:],
    )


def multiply_passes(nc, psum, stage, ident, acc, operands):
    passes = []
    for w_words, act_codes, act_planes in operands:
        for g in range(H_PASSES):
            w_codes = stage.tile([P, N_BLOCK], U32, tag="w_codes", bufs=4, align_bytes=64)
            w_plane = stage.tile([P, N_BLOCK], U8, tag="w_plane", bufs=4, align_bytes=64)
            quantise_weight_pass(
                nc, psum, stage, ident,
                w_words[:, :, g * PASS_WORDS : (g + 1) * PASS_WORDS], w_codes[:], w_plane[:],
            )
            passes.append((act_codes[:, g, :], act_planes[:, g, :], w_codes, w_plane))
    for i, (a_codes, a_plane, w_codes, w_plane) in enumerate(passes):
        nc.tensor.matmul_mx(
            out=acc[:],
            lhsT=a_codes.bitcast(FP8X4),
            lhsT_scale=a_plane,
            rhs=w_codes[:].bitcast(FP8X4),
            rhs_scale=w_plane[:],
            start=(i == 0),
            stop=(i == len(passes) - 1),
        )


def tile_decoderlstm_pa_kernel(
    tc, x, enc_seq, attn_W, attn_b, h_prev, c_prev, W_ih0, W_hh0, b_ih0, b_hh0, out_0, out_1
):
    nc = tc.nc
    with ExitStack() as stack:
        const = stack.enter_context(tc.tile_pool(name="const", bufs=1))
        keep = stack.enter_context(tc.tile_pool(name="keep", bufs=1))
        stage = stack.enter_context(tc.tile_pool(name="stage", bufs=2))
        work = stack.enter_context(tc.tile_pool(name="work", bufs=2))
        psum = stack.enter_context(tc.psum_pool(name="psum", bufs=2))

        def load_enc_group(group):
            enc = work.tile([P, S, GROUP], BF16, tag="enc")
            feats = slice(group * GROUP, (group + 1) * GROUP)
            for i in range(S // QUARTER):
                steps = slice(i * QUARTER, (i + 1) * QUARTER)
                nc.sync.dma_start(out=enc[:, steps, :], in_=enc_seq[steps, :, feats].rearrange("s b j -> b s j"))
            return enc

        ident = const.tile([P, P], F32)
        make_identity(nc, ident[:])
        ones = const.tile([P, P], BF16)
        nc.vector.memset(ones[:], 1.0)

        enc_groups = [load_enc_group(0)]
        x_sb = stage.tile([P, H], BF16, tag="w_rows", bufs=4)
        nc.sync.dma_start(out=x_sb[:], in_=x)
        attn_w_words = [
            load_weight_rows(nc, stage, attn_W[nb * N_BLOCK : (nb + 1) * N_BLOCK, :]) for nb in range(H_BLOCKS)
        ]
        bias_rows = work.tile([P, 5 * H], BF16, tag="exps")
        nc.vector.memset(bias_rows[:].bitcast(I32), 0)
        nc.sync.dma_start(out=bias_rows[0:1, 4 * H : 5 * H], in_=attn_b.rearrange("(o n) -> o n", o=1))
        nc.sync.dma_start(out=bias_rows[0:1, 0 : 4 * H], in_=b_ih0.rearrange("(o n) -> o n", o=1))
        nc.sync.dma_start(out=bias_rows[1:2, 0 : 4 * H], in_=b_hh0.rearrange("(o n) -> o n", o=1))
        h_sb = stage.tile([P, H], BF16, tag="w_rows", bufs=4)
        nc.sync.dma_start(out=h_sb[:], in_=h_prev)
        c_sb = keep.tile([P, H], BF16)
        nc.sync.dma_start(out=c_sb[:], in_=c_prev)

        x_codes = keep.tile([P, H_PASSES, P], U32, align_bytes=64)
        x_planes = keep.tile([P, H_PASSES, P], U8, align_bytes=64)
        quantise_activations(nc, psum, stage, ident, x_sb, x_codes, x_planes)
        h_codes = keep.tile([P, H_PASSES, P], U32, align_bytes=64)
        h_planes = keep.tile([P, H_PASSES, P], U8, align_bytes=64)
        quantise_activations(nc, psum, stage, ident, h_sb, h_codes, h_planes)

        attn_lin = keep.tile([P, H], F32)
        for nb in range(H_BLOCKS):
            cols = slice(nb * N_BLOCK, (nb + 1) * N_BLOCK)
            spread = psum.tile([P, N_BLOCK], F32, tag="acc")
            nc.tensor.matmul(
                out=spread[:], lhsT=ones[:], rhs=bias_rows[:, 4 * H + nb * N_BLOCK : 4 * H + (nb + 1) * N_BLOCK],
                start=True, stop=True,
            )
            nc.scalar.copy(out=attn_lin[:, cols], in_=spread[:])
            acc = psum.tile([P, N_BLOCK], F32, tag="acc")
            multiply_passes(nc, psum, stage, ident, acc, [(attn_w_words[nb], x_codes, x_planes)])
            nc.vector.tensor_tensor(out=attn_lin[:, cols], in0=acc[:], in1=attn_lin[:, cols], op=ALU.add)

        gates_xh = keep.tile([P, 4 * H], F32)
        for nb in range(GATE_BLOCKS):
            cols = slice(nb * N_BLOCK, (nb + 1) * N_BLOCK)
            spread = psum.tile([P, N_BLOCK], F32, tag="acc")
            nc.tensor.matmul(out=spread[:], lhsT=ones[:], rhs=bias_rows[:, cols], start=True, stop=True)
            nc.scalar.copy(out=gates_xh[:, cols], in_=spread[:])

        wa_codes = keep.tile([P, GATE_BLOCKS, H_PASSES, N_BLOCK], U32, align_bytes=64)
        wa_planes = keep.tile([P, GATE_BLOCKS, H_PASSES, N_BLOCK], U8, align_bytes=64)
        att_codes = keep.tile([P, H_PASSES, P], U32, align_bytes=64)
        att_planes = keep.tile([P, H_PASSES, P], U8, align_bytes=64)

        def gate_block(nb):
            rows = slice(nb * N_BLOCK, (nb + 1) * N_BLOCK)
            wx_words = load_weight_rows(nc, stage, W_ih0[rows, 0:H])
            wh_words = load_weight_rows(nc, stage, W_hh0[rows, :])
            wa_words = load_weight_rows(nc, stage, W_ih0[rows, H : 2 * H])
            acc = psum.tile([P, N_BLOCK], F32, tag="acc")
            multiply_passes(
                nc, psum, stage, ident, acc, [(wx_words, x_codes, x_planes), (wh_words, h_codes, h_planes)]
            )
            nc.vector.tensor_tensor(out=gates_xh[:, rows], in0=acc[:], in1=gates_xh[:, rows], op=ALU.add)
            for g in range(H_PASSES):
                quantise_weight_pass(
                    nc, psum, stage, ident,
                    wa_words[:, :, g * PASS_WORDS : (g + 1) * PASS_WORDS],
                    wa_codes[:, nb, g, :], wa_planes[:, nb, g, :],
                )

        def negated_peaks(group):
            enc = enc_groups[group]
            feats = slice(group * GROUP, (group + 1) * GROUP)
            top = work.tile([P, QUARTER, GROUP], BF16, tag="top", bufs=1)
            low = work.tile([P, QUARTER, GROUP], BF16, tag="low", bufs=1)
            nc.vector.tensor_tensor(out=top[:], in0=enc[:, 0:QUARTER, :], in1=enc[:, QUARTER : 2 * QUARTER, :], op=ALU.max)
            nc.vector.tensor_tensor(out=low[:], in0=enc[:, 0:QUARTER, :], in1=enc[:, QUARTER : 2 * QUARTER, :], op=ALU.min)
            for i in range(2, S // QUARTER):
                steps = slice(i * QUARTER, (i + 1) * QUARTER)
                nc.vector.tensor_tensor(out=top[:], in0=top[:], in1=enc[:, steps, :], op=ALU.max)
                nc.vector.tensor_tensor(out=low[:], in0=low[:], in1=enc[:, steps, :], op=ALU.min)
            half = QUARTER // 2
            while half >= 1:
                nc.vector.tensor_tensor(out=top[:, 0:half, :], in0=top[:, 0:half, :], in1=top[:, half : 2 * half, :], op=ALU.max)
                nc.vector.tensor_tensor(out=low[:, 0:half, :], in0=low[:, 0:half, :], in1=low[:, half : 2 * half, :], op=ALU.min)
                half //= 2
            neg_top = work.tile([P, GROUP], F32, tag="neg_top", bufs=1)
            neg_low = work.tile([P, GROUP], F32, tag="neg_low", bufs=1)
            neg_peak = work.tile([P, GROUP], F32, tag="neg_peak")
            nc.vector.scalar_tensor_tensor(
                out=neg_top[:], in0=attn_lin[:, feats], scalar=-1.0, in1=top[:, 0, :], op0=ALU.mult, op1=ALU.mult
            )
            nc.vector.scalar_tensor_tensor(
                out=neg_low[:], in0=attn_lin[:, feats], scalar=-1.0, in1=low[:, 0, :], op0=ALU.mult, op1=ALU.mult
            )
            nc.vector.tensor_tensor(out=neg_peak[:], in0=neg_top[:], in1=neg_low[:], op=ALU.min)
            return neg_peak

        def chunk_of(group, e):
            return enc_groups[group][:].rearrange("b s (p e) -> b s e p", e=2)[:, :, e, :]

        def sum_over_s(total, tiles, part):
            for i in range(S_HALF):
                s = part * S_HALF + i
                nc.tensor.matmul(
                    out=total[:], lhsT=tiles[:, i, :], rhs=ident[:], is_transpose=True,
                    start=(s == 0), stop=(s == S - 1),
                )

        def exponentials_by_scalar(group, neg_peak):
            enc = enc_groups[group]
            exps = work.tile([P, P, S], F32, tag="exps")
            exp_sum = work.tile([P, P], F32, tag="exp_sum")
            for p in range(P):
                j = 2 * p + 1
                nc.scalar.activation(
                    out=exps[:, p, :],
                    in_=enc[:, :, j],
                    func=ACT.Exp,
                    scale=attn_lin[:, group * GROUP + j : group * GROUP + j + 1],
                    bias=neg_peak[:, j : j + 1],
                    accum_out=exp_sum[:, p : p + 1],
                )
            exp_total = psum.tile([P, P], F32, tag="sums", bufs=3)
            nc.tensor.transpose(exp_total[:], exp_sum[:], ident[:])
            return exps[:].rearrange("b p s -> b s p"), exp_total

        def exponentials_by_vector(group, e, neg_peak):
            feats = slice(group * GROUP, (group + 1) * GROUP)
            lin_c = attn_lin[:, feats].rearrange("b (p e) -> b e p", e=2)[:, e, :]
            neg_peak_c = neg_peak[:].rearrange("b (p e) -> b e p", e=2)[:, e, :]
            exps = work.tile([P, S, P], F32, tag="exps")
            exp_total = psum.tile([P, P], F32, tag="sums", bufs=3)
            for part in range(HALVES):
                steps = slice(part * S_HALF, (part + 1) * S_HALF)
                nc.vector.tensor_tensor(
                    out=exps[:, steps, :], in0=chunk_of(group, e)[:, steps, :],
                    in1=lin_c.unsqueeze(1).to_broadcast([P, S_HALF, P]), op=ALU.mult,
                )
            for part in range(HALVES):
                steps = slice(part * S_HALF, (part + 1) * S_HALF)
                nc.vector.tensor_tensor(
                    out=exps[:, steps, :], in0=exps[:, steps, :],
                    in1=neg_peak_c.unsqueeze(1).to_broadcast([P, S_HALF, P]), op=ALU.add,
                )
                nc.scalar.activation(out=exps[:, steps, :], in_=exps[:, steps, :], func=ACT.Exp)
                sum_over_s(exp_total, exps[:, steps, :], part)
            return exps, exp_total

        def weighted_mean(enc_c, exps_bsp, exp_total, mean, s_is_innermost):
            inverse = work.tile([P, P], F32, tag="inverse")
            nc.vector.reciprocal(out=inverse[:], in_=exp_total[:])
            total = psum.tile([P, P], F32, tag="sums", bufs=3)
            for part in range(HALVES):
                steps = slice(part * S_HALF, (part + 1) * S_HALF)
                terms = work.tile([P, S_HALF, P], F32, tag="terms", bufs=3)
                if s_is_innermost:
                    nc.vector.tensor_tensor(
                        out=terms[:].rearrange("b (h l) p -> b h p l", l=2),
                        in0=exps_bsp[:, steps, :].rearrange("b (h l) p -> b h p l", l=2),
                        in1=enc_c[:, steps, :].rearrange("b (h l) p -> b h p l", l=2),
                        op=ALU.mult,
                    )
                else:
                    nc.vector.tensor_tensor(out=terms[:], in0=exps_bsp[:, steps, :], in1=enc_c[:, steps, :], op=ALU.mult)
                sum_over_s(total, terms, part)
            nc.vector.tensor_tensor(out=mean, in0=total[:], in1=inverse[:], op=ALU.mult)
            return inverse

        neg_peak = negated_peaks(0)
        for group in range(GROUPS):
            g, u = divmod(group, 2)
            if u == 0:
                att_t = work.tile([P, 4, P], F32, tag="att_t")
            gate_block(2 * group)
            gate_block(2 * group + 1)

            exps, exp_total = exponentials_by_vector(group, 0, neg_peak)
            weighted_mean(chunk_of(group, 0), exps, exp_total, att_t[:, 2 * u, :], s_is_innermost=False)

            if group + 1 < GROUPS:
                enc_groups.append(load_enc_group(group + 1))
                neg_peak_next = negated_peaks(group + 1)
            exps, exp_total = exponentials_by_scalar(group, neg_peak)
            inverse = weighted_mean(chunk_of(group, 1), exps, exp_total, att_t[:, 2 * u + 1, :], s_is_innermost=True)
            neg_peak = neg_peak_next

            if u == 1:
                att_grouped = work.tile([P, P, 4], BF16, tag="att_grouped", align_bytes=64)
                nc.vector.tensor_copy(out=att_grouped[:], in_=att_t[:].rearrange("p t b -> p b t"))
                nc.vector.quantize_mx(
                    out=att_codes[:, g, :].bitcast(FP8X4),
                    scales=att_planes[:, g, :],
                    in_=att_grouped[:].rearrange("p b t -> p (b t)"),
                )

        warm = work.tile([P, 1], F32, tag="warm", bufs=1)
        nc.scalar.activation(out=warm[:], in_=inverse[:, 0:1], func=ACT.Sigmoid)

        for part in range(H_BLOCKS):
            cols = slice(part * N_BLOCK, (part + 1) * N_BLOCK)
            cell = work.tile([P, 8, N_BLOCK], F32, tag="exps")
            for gate in range(4):
                nb = gate * H_BLOCKS + part
                acc = psum.tile([P, N_BLOCK], F32, tag="acc")
                for g in range(H_PASSES):
                    nc.tensor.matmul_mx(
                        out=acc[:],
                        lhsT=att_codes[:, g, :].bitcast(FP8X4),
                        lhsT_scale=att_planes[:, g, :],
                        rhs=wa_codes[:, nb, g, :].bitcast(FP8X4),
                        rhs_scale=wa_planes[:, nb, g, :],
                        start=(g == 0),
                        stop=(g == H_PASSES - 1),
                    )
                nc.vector.tensor_tensor(
                    out=cell[:, gate, :], in0=acc[:], in1=gates_xh[:, nb * N_BLOCK : (nb + 1) * N_BLOCK], op=ALU.add
                )
                nc.scalar.activation(
                    out=cell[:, gate, :], in_=cell[:, gate, :], func=(ACT.Tanh if gate == 2 else ACT.Sigmoid)
                )
            gate_i, gate_f, gate_g, gate_o = [cell[:, gate, :] for gate in range(4)]
            kept, c_new, tanh_c, h_new = [cell[:, 4 + i, :] for i in range(4)]
            nc.vector.tensor_tensor(out=kept, in0=gate_f, in1=c_sb[:, cols], op=ALU.mult)
            nc.vector.tensor_tensor(out=c_new, in0=gate_i, in1=gate_g, op=ALU.mult)
            nc.vector.tensor_tensor(out=c_new, in0=c_new, in1=kept, op=ALU.add)
            nc.sync.dma_start(out=out_1[:, cols], in_=c_new)
            nc.scalar.activation(out=tanh_c, in_=c_new, func=ACT.Tanh)
            nc.vector.tensor_tensor(out=h_new, in0=gate_o, in1=tanh_c, op=ALU.mult)
            nc.sync.dma_start(out=out_0[:, cols], in_=h_new)
